import numpy as np
import ml_dtypes


def mxq(x, axis, fmt="e4m3"):
    dtype, down = {"e4m3": (ml_dtypes.float8_e4m3fn, 7), "e5m2": (ml_dtypes.float8_e5m2, 14)}[fmt]
    v = np.moveaxis(np.asarray(x, np.float32).astype(ml_dtypes.bfloat16).astype(np.float64), axis, -1)
    blocks = v.reshape(v.shape[:-1] + (-1, 32))
    amax = np.abs(blocks).max(-1, keepdims=True)
    byte = np.maximum(np.where(amax > 0, np.frexp(amax)[1] - 1 + 127, 0) - down, 1)
    scale = np.exp2(byte - 127.0)
    codes = (blocks / scale).astype(np.float32).astype(dtype).astype(np.float64)
    return np.moveaxis((codes * scale).reshape(v.shape), -1, axis)


WIDE = False


def mx_kscale(k):
    if not WIDE:
        return np.ones(k)
    levels = np.array([30, -30])
    if k % 512:
        return np.exp2(np.random.permutation(np.resize(levels, k // 32))).repeat(32)
    a = np.empty((k // 512, 16))
    for p in range(k // 512):
        a[p, :8] = np.random.permutation(np.resize(levels, 8))
        for g in range(8):
            far = levels[np.abs(levels - a[p, g]) >= 10]
            a[p, g + 8] = far[np.random.randint(len(far))]
    return np.exp2(a.ravel()).repeat(32)


BF16 = ml_dtypes.bfloat16


def bf(x):
    return np.asarray(x, np.float32).astype(BF16)


def f64(x):
    return np.asarray(x).astype(np.float64)


B, T, C, H, D = 2, 512, 1024, 8, 128
HD = H * D
EPS = 2.0 ** -23
ROPE_BASE = 2.0 ** 10
BOUND = np.sqrt(3.0) * 0.5 / np.sqrt(C)


def rope_tables():
    freq = np.concatenate([(1.0 / ROPE_BASE) ** np.linspace(0.0, 1.0, D // 4), np.zeros(D // 4)])
    theta = f64(np.arange(T))[:, None] * freq[None, :]
    return np.cos(theta), np.sin(theta)


def apply_rope(u, cos, sin):
    u1, u2 = u[..., : D // 2], u[..., D // 2 :]
    c, s = cos[None, :, None, :], sin[None, :, None, :]
    return np.concatenate([u1 * c + u2 * s, u2 * c - u1 * s], axis=-1)


def rms_norm(u):
    return u / np.sqrt(np.mean(np.square(u), axis=-1, keepdims=True) + EPS)


def setup_inputs():
    s = mx_kscale(C)
    return {"x": bf(np.random.standard_normal((B, T, C)) * s),
            "ve": bf(np.random.standard_normal((B, T, HD))),
            "qkv_w": bf(np.random.uniform(-BOUND, BOUND, (3, HD, C)) / s),
            "lambdas": bf(0.5 + 0.1 * np.random.standard_normal(2))}


def reference(x, ve, qkv_w, lambdas):
    w = f64(qkv_w).reshape(3 * HD, C)
    qkv = (mxq(f64(x), 2, "e5m2") @ mxq(w, 1, "e5m2").T).reshape(B, T, 3, H, D)
    q, k, v = qkv[:, :, 0], qkv[:, :, 1], qkv[:, :, 2]
    cos, sin = rope_tables()
    q = apply_rope(rms_norm(q), cos, sin)
    k = apply_rope(rms_norm(k), cos, sin)
    lam = f64(lambdas)
    v = lam[0] * v + lam[1] * f64(ve).reshape(B, T, H, D)
    return q, k, v

@@ -1,0 +1,286 @@
+import math
+from contextlib import ExitStack
+
+import concourse.mybir as mybir
+from concourse.masks import make_identity
+
+F32 = mybir.dt.float32
+BF16 = mybir.dt.bfloat16
+I32 = mybir.dt.int32
+U32 = mybir.dt.uint32
+U8 = mybir.dt.uint8
+E5M2X4 = mybir.dt.float8_e5m2_x4
+ALU = mybir.AluOpType
+ACT = mybir.ActivationFunctionType
+
+P = 128
+TOKENS, SEQ, C, D = 1024, 512, 1024, 128
+N_TILE = 512
+HEADS = N_TILE // D
+ROT = D // 4
+M_TILES = TOKENS // P
+SEQ_TILES = SEQ // P
+PASSES = C // 512
+EPS = 2.0 ** -23
+ROPE_BASE = 2.0 ** 10
+FLOPS = 2 * TOKENS * C * 3 * C
+
+Q0, Q1, K0, K1, V0, V1 = range(6)
+
+
+def tile_causalselfattention_pa_kernel(tc, x, ve, qkv_w, lambdas, out_0, out_1, out_2):
+    nc = tc.nc
+    x_rows = x.rearrange("b t c -> (b t) c")
+    ve_rows = ve.rearrange("b t c -> (b t) c")
+    w_rows = qkv_w.rearrange("a n c -> (a n) c")
+    outs = [o.rearrange("b t h d -> (b t) (h d)") for o in (out_0, out_1, out_2)]
+
+    with ExitStack() as ctx:
+        keep = ctx.enter_context(tc.tile_pool(name="keep", bufs=1))
+        work = ctx.enter_context(tc.tile_pool(name="work", bufs=4))
+        res = ctx.enter_context(tc.tile_pool(name="res", bufs=16))
+        psum = ctx.enter_context(tc.psum_pool(name="psum", bufs=1))
+        ctx.enter_context(tc.manual_schedule())
+
+        banks_used = []
+
+        def new_bank():
+            name = "bank%d" % (len(banks_used) % 8)
+            bank = psum.tile([P, N_TILE], F32, name=name, tag=name)
+            banks_used.append(name)
+            return bank
+
+        x_raw = keep.tile([P, M_TILES, C], BF16, align_bytes=64)
+        ve_raw = keep.tile([P, M_TILES, C], BF16, align_bytes=64)
+        w_raw = keep.tile([P, 6 * HEADS, C], BF16, align_bytes=64)
+        lam = keep.tile([P, 2], BF16)
+        x_codes = keep.tile([P, M_TILES, PASSES * P], U32, align_bytes=64)
+        x_scales = keep.tile([P, M_TILES, PASSES * P], U8, align_bytes=64)
+        w_codes = keep.tile([P, 6, PASSES, N_TILE], U32, align_bytes=64)
+        w_scales = keep.tile([P, 6, PASSES, N_TILE], U8, align_bytes=64)
+
+        def load(dst, rows, r0, count):
+            nc.sync.dma_start(out=dst[:, r0 : r0 + count, :],
+                              in_=rows[r0 * P : (r0 + count) * P, :].rearrange("(r p) k -> p r k", p=P))
+
+        load(w_raw, w_rows, 0, 2)
+        load(x_raw, x_rows, 0, 1)
+        load(w_raw, w_rows, 2, 2)
+        load(x_raw, x_rows, 1, 1)
+        load(x_raw, x_rows, 2, 2)
+        load(x_raw, x_rows, 4, 2)
+        load(x_raw, x_rows, 6, 2)
+        load(w_raw, w_rows, Q1 * HEADS, HEADS)
+        load(w_raw, w_rows, V0 * HEADS, HEADS)
+        nc.sync.dma_start(out=lam[:], in_=lambdas.partition_broadcast(P))
+        load(w_raw, w_rows, K0 * HEADS, HEADS)
+        load(ve_raw, ve_rows, 0, 4)
+        load(ve_raw, ve_rows, 4, 4)
+        load(w_raw, w_rows, V1 * HEADS, HEADS)
+        load(w_raw, w_rows, K1 * HEADS, HEADS)
+
+        pos = keep.tile([P, SEQ_TILES], F32)
+        nc.gpsimd.iota(pos[:], [[P, SEQ_TILES]], base=0, channel_multiplier=1, allow_small_or_imprecise_dtypes=True)
+        ident = keep.tile([P, P], F32)
+        make_identity(nc, ident[:])
+        eps = keep.tile([P, 1], F32)
+        nc.gpsimd.memset(eps[:], EPS)
+        perm = keep.tile([P, P], F32)
+        nc.vector.tensor_copy(out=perm[:].rearrange("p (a b i) -> p a b i", a=2, b=2),
+                              in_=ident[:].rearrange("p (b a i) -> p a b i", a=2, b=2))
+
+        turns = keep.tile([P, 2, SEQ_TILES, ROT], F32)
+        ratio = (1.0 / ROPE_BASE) ** (1.0 / (ROT - 1))
+        nc.vector.tensor_scalar(out=turns[:, 1, :, 0], in0=pos[:], scalar1=1.0 / (2.0 * math.pi), scalar2=None, op0=ALU.mult)
+        width = 1
+        while width < ROT:
+            nc.vector.tensor_scalar(out=turns[:, 1, :, width : 2 * width], in0=turns[:, 1, :, 0:width],
+                                    scalar1=ratio ** width, scalar2=None, op0=ALU.mult)
+            width *= 2
+        nc.vector.tensor_scalar(out=turns[:, 0], in0=turns[:, 1], scalar1=0.25, scalar2=None, op0=ALU.add)
+        turns_flat = turns[:].rearrange("p a j i -> p (a j i)")
+        whole = keep.tile([P, 2 * SEQ_TILES * ROT], I32)
+        nc.vector.tensor_copy(out=whole[:], in_=turns_flat)
+        frac = keep.tile([P, 2 * SEQ_TILES * ROT], F32)
+        nc.vector.tensor_tensor(out=frac[:], in0=turns_flat, in1=whole[:], op=ALU.subtract)
+        neg = keep.tile([P, 2, SEQ_TILES, ROT], F32)
+        nc.vector.scalar_tensor_tensor(out=neg[:].rearrange("p a j i -> p (a j i)"), in0=frac[:], scalar=0.5, in1=frac[:],
+                                       op0=ALU.is_gt, op1=ALU.subtract)
+        table = keep.tile([P, SEQ_TILES, 4, ROT], F32)
+        for slot, (row, sign) in enumerate(((0, -1.0), (0, -1.0), (1, 1.0), (1, -1.0))):
+            nc.scalar.activation(out=table[:, :, slot, :], in_=neg[:, row], func=ACT.Sin, scale=sign * 2.0 * math.pi)
+
+        def x_unit(m):
+            return [(x_raw[:, m, :], g) for g in range(PASSES)], ident, x_codes[:, m, :], x_scales[:, m, :]
+
+        def w_unit(n, half, g):
+            cols = slice(half * 2 * P, (half + 1) * 2 * P)
+            return ([(w_raw[:, n * HEADS + 2 * half + r, :], g) for r in range(2)], ident if n >= V0 else perm,
+                    w_codes[:, n, g, cols], w_scales[:, n, g, cols])
+
+        def w_half(n, half):
+            return [w_unit(n, half, g) for g in range(PASSES)]
+
+        def transpose_unit(unit):
+            bank = new_bank()
+            for s, (rows, g) in enumerate(unit[0]):
+                words = rows.bitcast(F32)
+                for u in range(2):
+                    nc.tensor.transpose(bank[:, (2 * s + u) * P : (2 * s + u + 1) * P],
+                                        words[:, 256 * g + u : 256 * (g + 1) : 2], unit[1][:])
+            return bank
+
+        def copy_unit(bank, on_scalar):
+            grouped = work.tile([P, 2 * N_TILE], BF16, align_bytes=64, tag="grouped", bufs=6)
+            dst = grouped[:].bitcast(F32).rearrange("p (s c u) -> p s c u", s=2, u=2)
+            src = bank[:].rearrange("p (s u c) -> p s c u", s=2, u=2)
+            if on_scalar:
+                nc.scalar.copy(out=dst, in_=src)
+            else:
+                nc.vector.tensor_copy(out=dst, in_=src)
+            return grouped
+
+        def quantize_unit(unit, grouped):
+            nc.vector.quantize_mx(out=unit[2].bitcast(E5M2X4), scales=unit[3], in_=grouped[:])
+
+        def multiply(n, m):
+            bank = new_bank()
+            for g in range(PASSES):
+                cols = slice(g * P, (g + 1) * P)
+                nc.tensor.matmul_mx(out=bank[:], lhsT=x_codes[:, m, cols].bitcast(E5M2X4), lhsT_scale=x_scales[:, m, cols],
+                                    rhs=w_codes[:, n, g, :].bitcast(E5M2X4), rhs_scale=w_scales[:, n, g, :],
+                                    start=(g == 0), stop=(g == PASSES - 1))
+            return bank
+
+        def store(n, m0, count, tile_ap):
+            cols = slice((n % 2) * N_TILE, (n % 2 + 1) * N_TILE)
+            nc.sync.dma_start(out=outs[n // 2][m0 * P : (m0 + count) * P, cols].rearrange("(r p) c -> p r c", p=P), in_=tile_ap)
+
+        def square(job, h):
+            nc.scalar.activation(out=job["junk"][:, h * D : (h + 1) * D], in_=job["bank"][:, h * D : (h + 1) * D],
+                                 func=ACT.Square, accum_out=job["ss"][:, h : h + 1])
+
+        def inverse_rms(job):
+            nc.scalar.activation(out=job["rstd"][:], in_=job["ss"][:], func=ACT.Abs_reciprocal_sqrt, scale=1.0 / D, bias=eps[:])
+
+        def plain_part(job, on_scalar):
+            dst = job["res"][:, job["r"], :].rearrange("p (h a b i) -> p h a b i", h=HEADS, a=2, b=2)[:, :, :, 1, :]
+            src = job["bank"][:].rearrange("p (h a b i) -> p h a b i", h=HEADS, a=2, b=2)[:, :, 1, :, :]
+            if on_scalar:
+                for h in range(HEADS):
+                    nc.scalar.activation(out=dst[:, h], in_=src[:, h], func=ACT.Copy, scale=job["rstd"][:, h : h + 1])
+            else:
+                scale = job["rstd"][:].rearrange("p (h a i) -> p h a i", a=1, i=1).to_broadcast([P, HEADS, 2, ROT])
+                nc.vector.tensor_tensor(out=dst, in0=src, in1=scale, op=ALU.mult)
+
+        def products(job):
+            for h in range(HEADS):
+                src = job["bank"][:, h * D : h * D + 2 * ROT].rearrange("p (a i) -> p a i", a=1).to_broadcast([P, 2, 2 * ROT])
+                nc.vector.scalar_tensor_tensor(
+                    out=job["prod"][:, job["r"] * HEADS + h, :].rearrange("p (a i) -> p a i", a=2), in0=src,
+                    scalar=job["rstd"][:, h : h + 1],
+                    in1=table[:, job["m"] % SEQ_TILES].rearrange("p (a b) i -> p a (b i)", a=2), op0=ALU.mult, op1=ALU.mult)
+
+        def rotate_sum(engine, job, r0, count):
+            heads = slice(r0 * HEADS, (r0 + count) * HEADS)
+            dst = job["res"][:].rearrange("p r (h d) -> p (r h) d", d=D)
+            prod = job["prod"]
+            engine.tensor_tensor(out=dst[:, heads, 0:ROT], in0=prod[:, heads, 0:ROT], in1=prod[:, heads, 3 * ROT : 4 * ROT], op=ALU.add)
+            engine.tensor_tensor(out=dst[:, heads, 2 * ROT : 3 * ROT], in0=prod[:, heads, ROT : 2 * ROT],
+                                 in1=prod[:, heads, 2 * ROT : 3 * ROT], op=ALU.add)
+
+        qk_pairs = [(n, m0) for n in (Q0, Q1, K0, K1) for m0 in range(0, M_TILES, 2)]
+        last = len(qk_pairs) - 1
+        units = [[] for i in qk_pairs]
+        units[0] = [x_unit(4), x_unit(5)]
+        units[1] = [x_unit(6), x_unit(7)] + w_half(Q1, 0)
+        units[2] = w_half(Q1, 1) + w_half(V0, 0)
+        for i, (n, half) in enumerate(((V0, 1), (K0, 0), (K0, 1), (V1, 0), (V1, 1), (K1, 0), (K1, 1))):
+            units[3 + i] = w_half(n, half)
+        v_counts = [0] * 5 + [1] * 5 + [2] * 5 + [1]
+        v_all = [(n, m) for n in (V0, V1) for m in range(M_TILES)]
+        v_jobs = [v_all[sum(v_counts[:i]) : sum(v_counts[: i + 1])] for i in range(len(qk_pairs))]
+        v_jobs.append([])
+
+        def plain_on_scalar(i):
+            return 10 <= i < last
+
+        head = w_half(Q0, 0) + [x_unit(0)] + w_half(Q0, 1) + [x_unit(1), x_unit(2), x_unit(3)]
+        waiting = []
+        for j, unit in enumerate(head):
+            grouped = copy_unit(transpose_unit(unit), j % 2 == 1 or j >= 5)
+            for args in waiting:
+                quantize_unit(*args)
+            waiting = [(unit, grouped)]
+
+        v_res = {}
+        ve_scaled = {}
+
+        def scale_ve(n, m):
+            scaled = work.tile([P, N_TILE], F32, tag="ve_scaled", bufs=4)
+            cols = slice((n % 2) * N_TILE, (n % 2 + 1) * N_TILE)
+            nc.gpsimd.tensor_scalar(out=scaled[:], in0=ve_raw[:, m, cols], scalar1=lam[:, 1:2], scalar2=0.0, op0=ALU.mult, op1=ALU.add)
+            ve_scaled[(n, m)] = scaled
+
+        def blend(n, m, bank):
+            if m % 2 == 0:
+                v_res[n] = res.tile([P, 2, N_TILE], F32, name="result", tag="result")
+            nc.vector.scalar_tensor_tensor(out=v_res[n][:, m % 2, :], in0=bank[:], scalar=lam[:, 0:1], in1=ve_scaled[(n, m)][:],
+                                           op0=ALU.mult, op1=ALU.add)
+            if m % 2 == 1:
+                store(n, m - 1, 2, v_res[n][:])
+
+        def finish(job):
+            i = job["i"]
+            if plain_on_scalar(i):
+                plain_part(job, True)
+            products(job)
+            if not plain_on_scalar(i):
+                plain_part(job, False)
+            if i == last:
+                rotate_sum(nc.vector, job, job["r"], 1)
+                store(job["n"], job["m"], 1, job["res"][:, job["r"] : job["r"] + 1, :])
+            elif job["r"] == 1:
+                rotate_sum(nc.gpsimd, job, 0, 2)
+                store(job["n"], job["m"] - 1, 2, job["res"][:])
+
+        pending = None
+        for i, (n, m0) in enumerate(qk_pairs):
+            v_banks = [multiply(*v) for v in v_jobs[i]]
+            result = res.tile([P, 2, N_TILE], F32, name="result", tag="result")
+            prod = work.tile([P, 2 * HEADS, D], F32, tag="prod", bufs=3)
+            jobs = []
+            for r in range(2):
+                junk = work.tile([P, N_TILE], F32, tag="junk", bufs=2)
+                ss = work.tile([P, HEADS], F32, tag="ss")
+                rstd = work.tile([P, HEADS], F32, tag="rstd")
+                jobs.append({"i": i, "n": n, "m": m0 + r, "r": r, "res": result, "prod": prod, "junk": junk, "ss": ss, "rstd": rstd})
+            if i == 0:
+                for args in waiting:
+                    quantize_unit(*args)
+                waiting = []
+            for job in jobs:
+                job_bank = multiply(n, job["m"])
+                job.update({"bank": job_bank})
+            for v, bank in zip(v_jobs[i], v_banks):
+                blend(v[0], v[1], bank)
+            for args in waiting:
+                quantize_unit(*args)
+            for v in v_jobs[i + 1]:
+                scale_ve(*v)
+            for job in jobs:
+                square(job, 0)
+                if pending is not None:
+                    inverse_rms(pending)
+                for h in range(1, HEADS):
+                    square(job, h)
+                if pending is not None:
+                    finish(pending)
+                pending = job
+            unit_banks = [transpose_unit(unit) for unit in units[i]]
+            waiting = []
+            for j, unit in enumerate(units[i]):
+                grouped = copy_unit(unit_banks[j], j < 3)
+                waiting.append((unit, grouped))
+        inverse_rms(pending)
+        finish(pending)

@@ -20,12 +20,20 @@ HEADS = N_TILE // D
 ROT = D // 4
 M_TILES = TOKENS // P
 SEQ_TILES = SEQ // P
-PASSES = C // 512
+K_PASS = 4 * P
+PASSES = C // K_PASS
 EPS = 2.0 ** -23
 ROPE_BASE = 2.0 ** 10
 FLOPS = 2 * TOKENS * C * 3 * C
 
 Q0, Q1, K0, K1, V0, V1 = range(6)
+RING = 4
+
+STEPS = 4 * M_TILES // 2
+DOUBLE_PART_STEPS = (2, 3)
+V_FIRST, V_DOUBLE = 5, 9
+DOUBLE_SCALE_STEPS = 3
+SCALAR_COPIES = 3
 
 
 def tile_causalselfattention_pa_kernel(tc, x, ve, qkv_w, lambdas, out_0, out_1, out_2):
@@ -38,16 +46,16 @@ def tile_causalselfattention_pa_kernel(tc, x, ve, qkv_w, lambdas, out_0, out_1, 
     with ExitStack() as ctx:
         keep = ctx.enter_context(tc.tile_pool(name="keep", bufs=1))
         work = ctx.enter_context(tc.tile_pool(name="work", bufs=4))
-        res = ctx.enter_context(tc.tile_pool(name="res", bufs=16))
+        res = ctx.enter_context(tc.tile_pool(name="res", bufs=10))
         psum = ctx.enter_context(tc.psum_pool(name="psum", bufs=1))
         ctx.enter_context(tc.manual_schedule())
 
-        banks_used = []
+        banks_taken = {"norm": [], "short": []}
 
-        def new_bank():
-            name = "bank%d" % (len(banks_used) % 8)
+        def new_bank(ring):
+            name = "%s%d" % (ring, len(banks_taken[ring]) % RING)
             bank = psum.tile([P, N_TILE], F32, name=name, tag=name)
-            banks_used.append(name)
+            banks_taken[ring].append(name)
             return bank
 
         x_raw = keep.tile([P, M_TILES, C], BF16, align_bytes=64)
@@ -58,24 +66,26 @@ def tile_causalselfattention_pa_kernel(tc, x, ve, qkv_w, lambdas, out_0, out_1, 
         x_scales = keep.tile([P, M_TILES, PASSES * P], U8, align_bytes=64)
         w_codes = keep.tile([P, 6, PASSES, N_TILE], U32, align_bytes=64)
         w_scales = keep.tile([P, 6, PASSES, N_TILE], U8, align_bytes=64)
+        v_res = keep.tile([P, M_TILES, 2, N_TILE], F32)
 
-        def load(dst, rows, r0, count):
-            nc.sync.dma_start(out=dst[:, r0 : r0 + count, :],
-                              in_=rows[r0 * P : (r0 + count) * P, :].rearrange("(r p) k -> p r k", p=P))
+        def load(dst, rows, tile0, count, cols=slice(0, C)):
+            nc.sync.dma_start(out=dst[:, tile0 : tile0 + count, cols],
+                              in_=rows[tile0 * P : (tile0 + count) * P, cols].rearrange("(r p) k -> p r k", p=P))
 
-        load(w_raw, w_rows, 0, 2)
+        for g in range(PASSES):
+            load(w_raw, w_rows, 0, 2, slice(g * K_PASS, (g + 1) * K_PASS))
         load(x_raw, x_rows, 0, 1)
         load(w_raw, w_rows, 2, 2)
         load(x_raw, x_rows, 1, 1)
         load(x_raw, x_rows, 2, 2)
+        nc.sync.dma_start(out=lam[:], in_=lambdas.partition_broadcast(P))
         load(x_raw, x_rows, 4, 2)
         load(x_raw, x_rows, 6, 2)
         load(w_raw, w_rows, Q1 * HEADS, HEADS)
+        load(ve_raw, ve_rows, 0, M_TILES // 2)
         load(w_raw, w_rows, V0 * HEADS, HEADS)
-        nc.sync.dma_start(out=lam[:], in_=lambdas.partition_broadcast(P))
         load(w_raw, w_rows, K0 * HEADS, HEADS)
-        load(ve_raw, ve_rows, 0, 4)
-        load(ve_raw, ve_rows, 4, 4)
+        load(ve_raw, ve_rows, M_TILES // 2, M_TILES // 2)
         load(w_raw, w_rows, V1 * HEADS, HEADS)
         load(w_raw, w_rows, K1 * HEADS, HEADS)
 
@@ -85,66 +95,89 @@ def tile_causalselfattention_pa_kernel(tc, x, ve, qkv_w, lambdas, out_0, out_1, 
         make_identity(nc, ident[:])
         eps = keep.tile([P, 1], F32)
         nc.gpsimd.memset(eps[:], EPS)
+        zeros = keep.tile([P, 2 * P], F32)
+        nc.vector.memset(zeros[:], 0.0)
+
+        turns = keep.tile([P, SEQ_TILES, ROT], F32)
+        ratio = (1.0 / ROPE_BASE) ** (1.0 / (ROT - 1))
+        for i in range(4):
+            nc.vector.tensor_scalar(out=turns[:, :, i], in0=pos[:], scalar1=ratio ** i / (2.0 * math.pi), scalar2=None,
+                                    op0=ALU.mult)
+        for i in range(4, ROT, 4):
+            nc.vector.tensor_scalar(out=turns[:, :, i : i + 4], in0=turns[:, :, 0:4], scalar1=ratio ** i, scalar2=None,
+                                    op0=ALU.mult)
+        turns_flat = turns[:].rearrange("p j i -> p (j i)")
+        shifts = (0.25, 0.0)
+        whole = keep.tile([P, 2, SEQ_TILES * ROT], I32)
+        for row in range(2):
+            nc.vector.tensor_scalar(out=whole[:, row], in0=turns_flat, scalar1=shifts[row], scalar2=None, op0=ALU.add)
         perm = keep.tile([P, P], F32)
         nc.vector.tensor_copy(out=perm[:].rearrange("p (a b i) -> p a b i", a=2, b=2),
                               in_=ident[:].rearrange("p (b a i) -> p a b i", a=2, b=2))
-
-        turns = keep.tile([P, 2, SEQ_TILES, ROT], F32)
-        ratio = (1.0 / ROPE_BASE) ** (1.0 / (ROT - 1))
-        nc.vector.tensor_scalar(out=turns[:, 1, :, 0], in0=pos[:], scalar1=1.0 / (2.0 * math.pi), scalar2=None, op0=ALU.mult)
-        width = 1
-        while width < ROT:
-            nc.vector.tensor_scalar(out=turns[:, 1, :, width : 2 * width], in0=turns[:, 1, :, 0:width],
-                                    scalar1=ratio ** width, scalar2=None, op0=ALU.mult)
-            width *= 2
-        nc.vector.tensor_scalar(out=turns[:, 0], in0=turns[:, 1], scalar1=0.25, scalar2=None, op0=ALU.add)
-        turns_flat = turns[:].rearrange("p a j i -> p (a j i)")
-        whole = keep.tile([P, 2 * SEQ_TILES * ROT], I32)
-        nc.vector.tensor_copy(out=whole[:], in_=turns_flat)
-        frac = keep.tile([P, 2 * SEQ_TILES * ROT], F32)
-        nc.vector.tensor_tensor(out=frac[:], in0=turns_flat, in1=whole[:], op=ALU.subtract)
-        neg = keep.tile([P, 2, SEQ_TILES, ROT], F32)
-        nc.vector.scalar_tensor_tensor(out=neg[:].rearrange("p a j i -> p (a j i)"), in0=frac[:], scalar=0.5, in1=frac[:],
-                                       op0=ALU.is_gt, op1=ALU.subtract)
+        frac = keep.tile([P, 2, SEQ_TILES * ROT], F32)
+        for row in range(2):
+            nc.vector.scalar_tensor_tensor(out=frac[:, row], in0=turns_flat, scalar=shifts[row], in1=whole[:, row],
+                                           op0=ALU.add, op1=ALU.subtract)
+        frac_flat = frac[:].rearrange("p a c -> p (a c)")
+        minus_frac = keep.tile([P, 2, SEQ_TILES, ROT], F32)
+        nc.vector.scalar_tensor_tensor(out=minus_frac[:].rearrange("p a j i -> p (a j i)"), in0=frac_flat, scalar=0.5,
+                                       in1=frac_flat, op0=ALU.is_gt, op1=ALU.subtract)
         table = keep.tile([P, SEQ_TILES, 4, ROT], F32)
-        for slot, (row, sign) in enumerate(((0, -1.0), (0, -1.0), (1, 1.0), (1, -1.0))):
-            nc.scalar.activation(out=table[:, :, slot, :], in_=neg[:, row], func=ACT.Sin, scale=sign * 2.0 * math.pi)
+        for place, (row, sign) in enumerate(((0, 1.0), (0, 1.0), (1, -1.0), (1, 1.0))):
+            nc.scalar.activation(out=table[:, :, place, :], in_=minus_frac[:, row], func=ACT.Sin, scale=-sign * 2.0 * math.pi)
 
-        def x_unit(m):
-            return [(x_raw[:, m, :], g) for g in range(PASSES)], ident, x_codes[:, m, :], x_scales[:, m, :]
+        unread = keep.tile([P, 1], F32)
+        nc.scalar.activation(out=unread[:], in_=eps[:], func=ACT.Abs_reciprocal_sqrt, scale=1.0 / D, bias=eps[:])
 
-        def w_unit(n, half, g):
-            cols = slice(half * 2 * P, (half + 1) * 2 * P)
-            return ([(w_raw[:, n * HEADS + 2 * half + r, :], g) for r in range(2)], ident if n >= V0 else perm,
-                    w_codes[:, n, g, cols], w_scales[:, n, g, cols])
+        def warm_up(count):
+            bank = new_bank("norm")
+            for c in range(count):
+                nc.tensor.matmul(out=bank[:, 0 : 2 * P], lhsT=zeros[:, 0:P], rhs=zeros[:], start=True, stop=True)
 
-        def w_half(n, half):
-            return [w_unit(n, half, g) for g in range(PASSES)]
+        def x_part(m0, count):
+            return {"banks": [[(x_raw[:, m, :], g) for g in range(PASSES)] for m in range(m0, m0 + count)],
+                    "order": ident,
+                    "codes": x_codes[:, m0 : m0 + count, :].rearrange("p m c -> p (m c)"),
+                    "scales": x_scales[:, m0 : m0 + count, :].rearrange("p m c -> p (m c)")}
 
-        def transpose_unit(unit):
-            bank = new_bank()
-            for s, (rows, g) in enumerate(unit[0]):
-                words = rows.bitcast(F32)
-                for u in range(2):
-                    nc.tensor.transpose(bank[:, (2 * s + u) * P : (2 * s + u + 1) * P],
-                                        words[:, 256 * g + u : 256 * (g + 1) : 2], unit[1][:])
-            return bank
+        def w_part(n, g, half0=0, count=2):
+            cols = slice(half0 * 2 * P, (half0 + count) * 2 * P)
+            return {"banks": [[(w_raw[:, n * HEADS + 2 * half + r, :], g) for r in range(2)]
+                              for half in range(half0, half0 + count)],
+                    "order": ident if n >= V0 else perm,
+                    "codes": w_codes[:, n, g, cols],
+                    "scales": w_scales[:, n, g, cols]}
 
-        def copy_unit(bank, on_scalar):
-            grouped = work.tile([P, 2 * N_TILE], BF16, align_bytes=64, tag="grouped", bufs=6)
-            dst = grouped[:].bitcast(F32).rearrange("p (s c u) -> p s c u", s=2, u=2)
+        def transpose_part(part):
+            banks = []
+            for pieces in part["banks"]:
+                bank = new_bank("short")
+                for s, (rows, g) in enumerate(pieces):
+                    words = rows.bitcast(F32)
+                    for u in range(2):
+                        nc.tensor.transpose(bank[:, (2 * s + u) * P : (2 * s + u + 1) * P],
+                                            words[:, 2 * P * g + u : 2 * P * (g + 1) : 2], part["order"][:])
+                banks.append(bank)
+            return banks
+
+        def new_staging():
+            staging = work.tile([P, 2, 2 * N_TILE], BF16, align_bytes=64, tag="staging")
+            return staging
+
+        def copy_bank(staging, j, bank, on_scalar):
+            dst = staging[:, j, :].bitcast(F32).rearrange("p (s c u) -> p s c u", s=2, u=2)
             src = bank[:].rearrange("p (s u c) -> p s c u", s=2, u=2)
             if on_scalar:
                 nc.scalar.copy(out=dst, in_=src)
             else:
                 nc.vector.tensor_copy(out=dst, in_=src)
-            return grouped
 
-        def quantize_unit(unit, grouped):
-            nc.vector.quantize_mx(out=unit[2].bitcast(E5M2X4), scales=unit[3], in_=grouped[:])
+        def quantize_part(part, staging):
+            nc.vector.quantize_mx(out=part["codes"].bitcast(E5M2X4), scales=part["scales"],
+                                  in_=staging[:, 0 : len(part["banks"]), :].rearrange("p j c -> p (j c)"))
 
         def multiply(n, m):
-            bank = new_bank()
+            bank = new_bank("short" if n >= V0 else "norm")
             for g in range(PASSES):
                 cols = slice(g * P, (g + 1) * P)
                 nc.tensor.matmul_mx(out=bank[:], lhsT=x_codes[:, m, cols].bitcast(E5M2X4), lhsT_scale=x_scales[:, m, cols],
@@ -152,19 +185,21 @@ def tile_causalselfattention_pa_kernel(tc, x, ve, qkv_w, lambdas, out_0, out_1, 
                                     start=(g == 0), stop=(g == PASSES - 1))
             return bank
 
-        def store(n, m0, count, tile_ap):
+        def store(n, m0, count, src):
             cols = slice((n % 2) * N_TILE, (n % 2 + 1) * N_TILE)
-            nc.sync.dma_start(out=outs[n // 2][m0 * P : (m0 + count) * P, cols].rearrange("(r p) c -> p r c", p=P), in_=tile_ap)
+            nc.sync.dma_start(out=outs[n // 2][m0 * P : (m0 + count) * P, cols].rearrange("(r p) c -> p r c", p=P), in_=src)
 
-        def square(job, h):
-            nc.scalar.activation(out=job["junk"][:, h * D : (h + 1) * D], in_=job["bank"][:, h * D : (h + 1) * D],
-                                 func=ACT.Square, accum_out=job["ss"][:, h : h + 1])
+        def sum_squares(job, heads):
+            for h in heads:
+                nc.scalar.activation(out=job["squares"][:, h * D : (h + 1) * D], in_=job["bank"][:, h * D : (h + 1) * D],
+                                     func=ACT.Square, accum_out=job["sums"][:, h : h + 1])
 
         def inverse_rms(job):
-            nc.scalar.activation(out=job["rstd"][:], in_=job["ss"][:], func=ACT.Abs_reciprocal_sqrt, scale=1.0 / D, bias=eps[:])
+            nc.scalar.activation(out=job["rstd"][:], in_=job["sums"][:], func=ACT.Abs_reciprocal_sqrt, scale=1.0 / D,
+                                 bias=eps[:])
 
-        def plain_part(job, on_scalar):
-            dst = job["res"][:, job["r"], :].rearrange("p (h a b i) -> p h a b i", h=HEADS, a=2, b=2)[:, :, :, 1, :]
+        def plain_half(job, on_scalar):
+            dst = job["result"][:, job["r"], :].rearrange("p (h a b i) -> p h a b i", h=HEADS, a=2, b=2)[:, :, :, 1, :]
             src = job["bank"][:].rearrange("p (h a b i) -> p h a b i", h=HEADS, a=2, b=2)[:, :, 1, :, :]
             if on_scalar:
                 for h in range(HEADS):
@@ -173,114 +208,114 @@ def tile_causalselfattention_pa_kernel(tc, x, ve, qkv_w, lambdas, out_0, out_1, 
                 scale = job["rstd"][:].rearrange("p (h a i) -> p h a i", a=1, i=1).to_broadcast([P, HEADS, 2, ROT])
                 nc.vector.tensor_tensor(out=dst, in0=src, in1=scale, op=ALU.mult)
 
-        def products(job):
+        def rope_products(job):
+            factors = table[:, job["m"] % SEQ_TILES].rearrange("p (a b) i -> p a (b i)", a=2)
             for h in range(HEADS):
                 src = job["bank"][:, h * D : h * D + 2 * ROT].rearrange("p (a i) -> p a i", a=1).to_broadcast([P, 2, 2 * ROT])
                 nc.vector.scalar_tensor_tensor(
-                    out=job["prod"][:, job["r"] * HEADS + h, :].rearrange("p (a i) -> p a i", a=2), in0=src,
-                    scalar=job["rstd"][:, h : h + 1],
-                    in1=table[:, job["m"] % SEQ_TILES].rearrange("p (a b) i -> p a (b i)", a=2), op0=ALU.mult, op1=ALU.mult)
+                    out=job["terms"][:, job["r"] * HEADS + h, :].rearrange("p (a i) -> p a i", a=2), in0=src,
+                    scalar=job["rstd"][:, h : h + 1], in1=factors, op0=ALU.mult, op1=ALU.mult)
 
-        def rotate_sum(engine, job, r0, count):
+        def rope_sums(engine, job, r0, count):
             heads = slice(r0 * HEADS, (r0 + count) * HEADS)
-            dst = job["res"][:].rearrange("p r (h d) -> p (r h) d", d=D)
-            prod = job["prod"]
-            engine.tensor_tensor(out=dst[:, heads, 0:ROT], in0=prod[:, heads, 0:ROT], in1=prod[:, heads, 3 * ROT : 4 * ROT], op=ALU.add)
-            engine.tensor_tensor(out=dst[:, heads, 2 * ROT : 3 * ROT], in0=prod[:, heads, ROT : 2 * ROT],
-                                 in1=prod[:, heads, 2 * ROT : 3 * ROT], op=ALU.add)
-
-        qk_pairs = [(n, m0) for n in (Q0, Q1, K0, K1) for m0 in range(0, M_TILES, 2)]
-        last = len(qk_pairs) - 1
-        units = [[] for i in qk_pairs]
-        units[0] = [x_unit(4), x_unit(5)]
-        units[1] = [x_unit(6), x_unit(7)] + w_half(Q1, 0)
-        units[2] = w_half(Q1, 1) + w_half(V0, 0)
-        for i, (n, half) in enumerate(((V0, 1), (K0, 0), (K0, 1), (V1, 0), (V1, 1), (K1, 0), (K1, 1))):
-            units[3 + i] = w_half(n, half)
-        v_counts = [0] * 5 + [1] * 5 + [2] * 5 + [1]
-        v_all = [(n, m) for n in (V0, V1) for m in range(M_TILES)]
-        v_jobs = [v_all[sum(v_counts[:i]) : sum(v_counts[: i + 1])] for i in range(len(qk_pairs))]
-        v_jobs.append([])
-
-        def plain_on_scalar(i):
-            return 10 <= i < last
-
-        head = w_half(Q0, 0) + [x_unit(0)] + w_half(Q0, 1) + [x_unit(1), x_unit(2), x_unit(3)]
-        waiting = []
-        for j, unit in enumerate(head):
-            grouped = copy_unit(transpose_unit(unit), j % 2 == 1 or j >= 5)
-            for args in waiting:
-                quantize_unit(*args)
-            waiting = [(unit, grouped)]
-
-        v_res = {}
-        ve_scaled = {}
+            dst = job["result"][:].rearrange("p r (h d) -> p (r h) d", d=D)
+            terms = job["terms"]
+            engine.tensor_tensor(out=dst[:, heads, 0:ROT], in0=terms[:, heads, 0:ROT], in1=terms[:, heads, 3 * ROT : 4 * ROT],
+                                 op=ALU.add)
+            engine.tensor_tensor(out=dst[:, heads, 2 * ROT : 3 * ROT], in0=terms[:, heads, ROT : 2 * ROT],
+                                 in1=terms[:, heads, 2 * ROT : 3 * ROT], op=ALU.add)
+            store(job["n"], job["m"] - job["r"] + r0, count, job["result"][:, r0 : r0 + count, :])
 
         def scale_ve(n, m):
-            scaled = work.tile([P, N_TILE], F32, tag="ve_scaled", bufs=4)
-            cols = slice((n % 2) * N_TILE, (n % 2 + 1) * N_TILE)
-            nc.gpsimd.tensor_scalar(out=scaled[:], in0=ve_raw[:, m, cols], scalar1=lam[:, 1:2], scalar2=0.0, op0=ALU.mult, op1=ALU.add)
-            ve_scaled[(n, m)] = scaled
+            nc.gpsimd.tensor_scalar(out=v_res[:, m, n % 2, :], in0=ve_raw[:, m, (n % 2) * N_TILE : (n % 2 + 1) * N_TILE],
+                                    scalar1=lam[:, 1:2], scalar2=0.0, op0=ALU.mult, op1=ALU.add)
 
         def blend(n, m, bank):
-            if m % 2 == 0:
-                v_res[n] = res.tile([P, 2, N_TILE], F32, name="result", tag="result")
-            nc.vector.scalar_tensor_tensor(out=v_res[n][:, m % 2, :], in0=bank[:], scalar=lam[:, 0:1], in1=ve_scaled[(n, m)][:],
-                                           op0=ALU.mult, op1=ALU.add)
+            nc.vector.scalar_tensor_tensor(out=v_res[:, m, n % 2, :], in0=bank[:], scalar=lam[:, 0:1],
+                                           in1=v_res[:, m, n % 2, :], op0=ALU.mult, op1=ALU.add)
             if m % 2 == 1:
-                store(n, m - 1, 2, v_res[n][:])
+                store(n, m - 1, 2, v_res[:, m - 1 : m + 1, n % 2, :])
+
+        parts_left = [x_part(4, 2), x_part(6, 2)] + [w_part(n, g) for n in (Q1, V0, K0, V1, K1) for g in range(PASSES)]
+        v_left = [(n, m) for n in (V0, V1) for m in range(M_TILES)]
+        ve_left = list(v_left)
+        staged = []
+
+        def take(items, count):
+            taken = items[0:count]
+            for item in taken:
+                items.remove(item)
+            return taken
 
         def finish(job):
-            i = job["i"]
-            if plain_on_scalar(i):
-                plain_part(job, True)
-            products(job)
-            if not plain_on_scalar(i):
-                plain_part(job, False)
-            if i == last:
-                rotate_sum(nc.vector, job, job["r"], 1)
-                store(job["n"], job["m"], 1, job["res"][:, job["r"] : job["r"] + 1, :])
-            elif job["r"] == 1:
-                rotate_sum(nc.gpsimd, job, 0, 2)
-                store(job["n"], job["m"] - 1, 2, job["res"][:])
+            step, second = job["step"], job["r"] == 1
+            on_scalar = second and job["no_copies"] and step < STEPS - 1
+            if on_scalar:
+                plain_half(job, True)
+            rope_products(job)
+            if second:
+                for part, staging in take(staged, len(staged)):
+                    quantize_part(part, staging)
+            if not on_scalar:
+                plain_half(job, False)
+            if step >= STEPS - 2:
+                rope_sums(nc.vector if step == STEPS - 1 else nc.gpsimd, job, job["r"], 1)
+            elif second:
+                rope_sums(nc.gpsimd, job, 0, 2)
+            if second:
+                for n, m in take(ve_left, 2 if step < DOUBLE_SCALE_STEPS else 1):
+                    scale_ve(n, m)
+
+        head = ([w_part(Q0, g, 0, 1) for g in range(PASSES)] + [x_part(0, 1)]
+                + [w_part(Q0, g, 1, 1) for g in range(PASSES)] + [x_part(m, 1) for m in (1, 2, 3)])
+        warm_ups = {0: 3, 3: 1, 5: 1}
+        for j, part in enumerate(head):
+            if j in warm_ups:
+                warm_up(warm_ups[j])
+            staging = new_staging()
+            copy_bank(staging, 0, transpose_part(part)[0], j % 2 == 1)
+            for earlier in take(staged, 1):
+                quantize_part(*earlier)
+            staged.append((part, staging))
+        quantize_part(*take(staged, 1)[0])
 
         pending = None
-        for i, (n, m0) in enumerate(qk_pairs):
-            v_banks = [multiply(*v) for v in v_jobs[i]]
+        pairs = [(n, m0) for n in (Q0, Q1, K0, K1) for m0 in range(0, M_TILES, 2)]
+        for step, (n, m0) in enumerate(pairs):
+            parts = take(parts_left, 2 if step in DOUBLE_PART_STEPS else 1)
+            v_tiles = take(v_left, 0 if step < V_FIRST else 1 if step < V_DOUBLE else 2)
             result = res.tile([P, 2, N_TILE], F32, name="result", tag="result")
-            prod = work.tile([P, 2 * HEADS, D], F32, tag="prod", bufs=3)
+            terms = work.tile([P, 2 * HEADS, D], F32, tag="terms", bufs=3)
             jobs = []
             for r in range(2):
-                junk = work.tile([P, N_TILE], F32, tag="junk", bufs=2)
-                ss = work.tile([P, HEADS], F32, tag="ss")
+                squares = work.tile([P, N_TILE], F32, tag="squares", bufs=2)
+                sums = work.tile([P, HEADS], F32, tag="sums")
                 rstd = work.tile([P, HEADS], F32, tag="rstd")
-                jobs.append({"i": i, "n": n, "m": m0 + r, "r": r, "res": result, "prod": prod, "junk": junk, "ss": ss, "rstd": rstd})
-            if i == 0:
-                for args in waiting:
-                    quantize_unit(*args)
-                waiting = []
+                jobs.append({"step": step, "n": n, "m": m0 + r, "r": r, "no_copies": not parts, "result": result,
+                             "terms": terms, "squares": squares, "sums": sums, "rstd": rstd, "bank": multiply(n, m0 + r)})
+            v_banks = [multiply(*v) for v in v_tiles]
             for job in jobs:
-                job_bank = multiply(n, job["m"])
-                job.update({"bank": job_bank})
-            for v, bank in zip(v_jobs[i], v_banks):
-                blend(v[0], v[1], bank)
-            for args in waiting:
-                quantize_unit(*args)
-            for v in v_jobs[i + 1]:
-                scale_ve(*v)
-            for job in jobs:
-                square(job, 0)
+                sum_squares(job, range(0, 1))
                 if pending is not None:
                     inverse_rms(pending)
-                for h in range(1, HEADS):
-                    square(job, h)
+                sum_squares(job, range(1, HEADS))
                 if pending is not None:
                     finish(pending)
                 pending = job
-            unit_banks = [transpose_unit(unit) for unit in units[i]]
-            waiting = []
-            for j, unit in enumerate(units[i]):
-                grouped = copy_unit(unit_banks[j], j < 3)
-                waiting.append((unit, grouped))
+            for v, bank in zip(v_tiles, v_banks):
+                blend(v[0], v[1], bank)
+            part_banks = [transpose_part(part) for part in parts]
+            copies = 0
+            for part, banks in zip(parts, part_banks):
+                staging = new_staging()
+                for j, bank in enumerate(banks):
+                    copy_bank(staging, j, bank, copies < SCALAR_COPIES)
+                    if copies == 0:
+                        inverse_rms(pending)
+                    copies += 1
+                staged.append((part, staging))
+            if parts:
+                finish(pending)
+                pending = None
         inverse_rms(pending)
         finish(pending)

@@ -38,10 +38,10 @@ SCALAR_COPIES = 3
 
 def tile_causalselfattention_pa_kernel(tc, x, ve, qkv_w, lambdas, out_0, out_1, out_2):
     nc = tc.nc
-    x_rows = x.rearrange("b t c -> (b t) c")
-    ve_rows = ve.rearrange("b t c -> (b t) c")
-    w_rows = qkv_w.rearrange("a n c -> (a n) c")
-    outs = [o.rearrange("b t h d -> (b t) (h d)") for o in (out_0, out_1, out_2)]
+    x_tiles = x.rearrange("b (p j) c -> p b j c", p=P)
+    ve_tiles = ve.rearrange("b (p j) c -> p b j c", p=P)
+    w_tiles = qkv_w.rearrange("a (r p) c -> p (a r) c", p=P)
+    outs = [o.rearrange("b (p j) h d -> p b j (h d)", p=P) for o in (out_0, out_1, out_2)]
 
     with ExitStack() as ctx:
         keep = ctx.enter_context(tc.tile_pool(name="keep", bufs=1))
@@ -68,29 +68,32 @@ def tile_causalselfattention_pa_kernel(tc, x, ve, qkv_w, lambdas, out_0, out_1, 
         w_scales = keep.tile([P, 6, PASSES, N_TILE], U8, align_bytes=64)
         v_res = keep.tile([P, M_TILES, 2, N_TILE], F32)
 
-        def load(dst, rows, tile0, count, cols=slice(0, C)):
-            nc.sync.dma_start(out=dst[:, tile0 : tile0 + count, cols],
-                              in_=rows[tile0 * P : (tile0 + count) * P, cols].rearrange("(r p) k -> p r k", p=P))
+        def load_tokens(dst, tiles, m0, count):
+            j0 = m0 % SEQ_TILES
+            nc.sync.dma_start(out=dst[:, m0 : m0 + count, :], in_=tiles[:, m0 // SEQ_TILES, j0 : j0 + count, :])
+
+        def load_weights(tile0, count, cols=slice(0, C)):
+            nc.sync.dma_start(out=w_raw[:, tile0 : tile0 + count, cols], in_=w_tiles[:, tile0 : tile0 + count, cols])
 
         for g in range(PASSES):
-            load(w_raw, w_rows, 0, 2, slice(g * K_PASS, (g + 1) * K_PASS))
-        load(x_raw, x_rows, 0, 1)
-        load(w_raw, w_rows, 2, 2)
-        load(x_raw, x_rows, 1, 1)
-        load(x_raw, x_rows, 2, 2)
+            load_weights(0, 2, slice(g * K_PASS, (g + 1) * K_PASS))
+        load_tokens(x_raw, x_tiles, 0, 1)
+        load_weights(2, 2)
+        load_tokens(x_raw, x_tiles, 1, 1)
+        load_tokens(x_raw, x_tiles, 2, 2)
         nc.sync.dma_start(out=lam[:], in_=lambdas.partition_broadcast(P))
-        load(x_raw, x_rows, 4, 2)
-        load(x_raw, x_rows, 6, 2)
-        load(w_raw, w_rows, Q1 * HEADS, HEADS)
-        load(ve_raw, ve_rows, 0, M_TILES // 2)
-        load(w_raw, w_rows, V0 * HEADS, HEADS)
-        load(w_raw, w_rows, K0 * HEADS, HEADS)
-        load(ve_raw, ve_rows, M_TILES // 2, M_TILES // 2)
-        load(w_raw, w_rows, V1 * HEADS, HEADS)
-        load(w_raw, w_rows, K1 * HEADS, HEADS)
+        load_tokens(x_raw, x_tiles, 4, 2)
+        load_tokens(x_raw, x_tiles, 6, 2)
+        load_weights(Q1 * HEADS, HEADS)
+        load_tokens(ve_raw, ve_tiles, 0, SEQ_TILES)
+        load_weights(V0 * HEADS, HEADS)
+        load_weights(K0 * HEADS, HEADS)
+        load_tokens(ve_raw, ve_tiles, SEQ_TILES, SEQ_TILES)
+        load_weights(V1 * HEADS, HEADS)
+        load_weights(K1 * HEADS, HEADS)
 
         pos = keep.tile([P, SEQ_TILES], F32)
-        nc.gpsimd.iota(pos[:], [[P, SEQ_TILES]], base=0, channel_multiplier=1, allow_small_or_imprecise_dtypes=True)
+        nc.gpsimd.iota(pos[:], [[1, SEQ_TILES]], base=0, channel_multiplier=SEQ_TILES, allow_small_or_imprecise_dtypes=True)
         ident = keep.tile([P, P], F32)
         make_identity(nc, ident[:])
         eps = keep.tile([P, 1], F32)
@@ -98,15 +101,15 @@ def tile_causalselfattention_pa_kernel(tc, x, ve, qkv_w, lambdas, out_0, out_1, 
         zeros = keep.tile([P, 2 * P], F32)
         nc.vector.memset(zeros[:], 0.0)
 
-        turns = keep.tile([P, SEQ_TILES, ROT], F32)
+        turns = keep.tile([P, ROT, SEQ_TILES], F32)
         ratio = (1.0 / ROPE_BASE) ** (1.0 / (ROT - 1))
         for i in range(4):
-            nc.vector.tensor_scalar(out=turns[:, :, i], in0=pos[:], scalar1=ratio ** i / (2.0 * math.pi), scalar2=None,
+            nc.vector.tensor_scalar(out=turns[:, i, :], in0=pos[:], scalar1=ratio ** i / (2.0 * math.pi), scalar2=None,
                                     op0=ALU.mult)
         for i in range(4, ROT, 4):
-            nc.vector.tensor_scalar(out=turns[:, :, i : i + 4], in0=turns[:, :, 0:4], scalar1=ratio ** i, scalar2=None,
+            nc.vector.tensor_scalar(out=turns[:, i : i + 4, :], in0=turns[:, 0:4, :], scalar1=ratio ** i, scalar2=None,
                                     op0=ALU.mult)
-        turns_flat = turns[:].rearrange("p j i -> p (j i)")
+        turns_flat = turns[:].rearrange("p i j -> p (i j)")
         shifts = (0.25, 0.0)
         whole = keep.tile([P, 2, SEQ_TILES * ROT], I32)
         for row in range(2):
@@ -119,12 +122,13 @@ def tile_causalselfattention_pa_kernel(tc, x, ve, qkv_w, lambdas, out_0, out_1, 
             nc.vector.scalar_tensor_tensor(out=frac[:, row], in0=turns_flat, scalar=shifts[row], in1=whole[:, row],
                                            op0=ALU.add, op1=ALU.subtract)
         frac_flat = frac[:].rearrange("p a c -> p (a c)")
-        minus_frac = keep.tile([P, 2, SEQ_TILES, ROT], F32)
-        nc.vector.scalar_tensor_tensor(out=minus_frac[:].rearrange("p a j i -> p (a j i)"), in0=frac_flat, scalar=0.5,
+        minus_frac = keep.tile([P, 2, ROT, SEQ_TILES], F32)
+        nc.vector.scalar_tensor_tensor(out=minus_frac[:].rearrange("p a i j -> p (a i j)"), in0=frac_flat, scalar=0.5,
                                        in1=frac_flat, op0=ALU.is_gt, op1=ALU.subtract)
         table = keep.tile([P, SEQ_TILES, 4, ROT], F32)
         for place, (row, sign) in enumerate(((0, 1.0), (0, 1.0), (1, -1.0), (1, 1.0))):
-            nc.scalar.activation(out=table[:, :, place, :], in_=minus_frac[:, row], func=ACT.Sin, scale=-sign * 2.0 * math.pi)
+            nc.scalar.activation(out=table[:, :, place, :], in_=minus_frac[:, row].rearrange("p i j -> p j i"),
+                                 func=ACT.Sin, scale=-sign * 2.0 * math.pi)
 
         unread = keep.tile([P, 1], F32)
         nc.scalar.activation(out=unread[:], in_=eps[:], func=ACT.Abs_reciprocal_sqrt, scale=1.0 / D, bias=eps[:])
@@ -187,7 +191,8 @@ def tile_causalselfattention_pa_kernel(tc, x, ve, qkv_w, lambdas, out_0, out_1, 
 
         def store(n, m0, count, src):
             cols = slice((n % 2) * N_TILE, (n % 2 + 1) * N_TILE)
-            nc.sync.dma_start(out=outs[n // 2][m0 * P : (m0 + count) * P, cols].rearrange("(r p) c -> p r c", p=P), in_=src)
+            j0 = m0 % SEQ_TILES
+            nc.sync.dma_start(out=outs[n // 2][:, m0 // SEQ_TILES, j0 : j0 + count, cols], in_=src)
 
         def sum_squares(job, heads):
             for h in heads:
@@ -249,7 +254,7 @@ def tile_causalselfattention_pa_kernel(tc, x, ve, qkv_w, lambdas, out_0, out_1, 
 
         def finish(job):
             step, second = job["step"], job["r"] == 1
-            on_scalar = second and job["no_copies"] and step < STEPS - 1
+            on_scalar = job["no_copies"] and not (second and step == STEPS - 1)
             if on_scalar:
                 plain_half(job, True)
             rope_products(job)
@@ -295,10 +300,10 @@ def tile_causalselfattention_pa_kernel(tc, x, ve, qkv_w, lambdas, out_0, out_1, 
                              "terms": terms, "squares": squares, "sums": sums, "rstd": rstd, "bank": multiply(n, m0 + r)})
             v_banks = [multiply(*v) for v in v_tiles]
             for job in jobs:
-                sum_squares(job, range(0, 1))
+                sum_squares(job, range(0, 2))
                 if pending is not None:
                     inverse_rms(pending)
-                sum_squares(job, range(1, HEADS))
+                sum_squares(job, range(2, HEADS))
                 if pending is not None:
                     finish(pending)
                 pending = job

import math
from contextlib import ExitStack

import concourse.mybir as mybir
from concourse.masks import make_identity

F32 = mybir.dt.float32
BF16 = mybir.dt.bfloat16
I32 = mybir.dt.int32
U32 = mybir.dt.uint32
U8 = mybir.dt.uint8
E5M2X4 = mybir.dt.float8_e5m2_x4
ALU = mybir.AluOpType
ACT = mybir.ActivationFunctionType

P = 128
TOKENS, SEQ, C, D = 1024, 512, 1024, 128
N_TILE = 512
HEADS = N_TILE // D
ROT = D // 4
M_TILES = TOKENS // P
SEQ_TILES = SEQ // P
K_PASS = 4 * P
PASSES = C // K_PASS
EPS = 2.0 ** -23
ROPE_BASE = 2.0 ** 10
FLOPS = 2 * TOKENS * C * 3 * C

Q0, Q1, K0, K1, V0, V1 = range(6)
RING = 4

STEPS = 4 * M_TILES // 2
DOUBLE_PART_STEPS = (2, 3)
V_FIRST, V_DOUBLE = 5, 9
DOUBLE_SCALE_STEPS = 3
SCALAR_COPIES = 3


def tile_causalselfattention_pa_kernel(tc, x, ve, qkv_w, lambdas, out_0, out_1, out_2):
    nc = tc.nc
    x_tiles = x.rearrange("b (p j) c -> p b j c", p=P)
    ve_tiles = ve.rearrange("b (p j) c -> p b j c", p=P)
    w_tiles = qkv_w.rearrange("a (r p) c -> p (a r) c", p=P)
    outs = [o.rearrange("b (p j) h d -> p b j (h d)", p=P) for o in (out_0, out_1, out_2)]

    with ExitStack() as ctx:
        keep = ctx.enter_context(tc.tile_pool(name="keep", bufs=1))
        work = ctx.enter_context(tc.tile_pool(name="work", bufs=4))
        res = ctx.enter_context(tc.tile_pool(name="res", bufs=10))
        psum = ctx.enter_context(tc.psum_pool(name="psum", bufs=1))
        ctx.enter_context(tc.manual_schedule())

        banks_taken = {"norm": [], "short": []}

        def new_bank(ring):
            name = "%s%d" % (ring, len(banks_taken[ring]) % RING)
            bank = psum.tile([P, N_TILE], F32, name=name, tag=name)
            banks_taken[ring].append(name)
            return bank

        x_raw = keep.tile([P, M_TILES, C], BF16, align_bytes=64)
        ve_raw = keep.tile([P, M_TILES, C], BF16, align_bytes=64)
        w_raw = keep.tile([P, 6 * HEADS, C], BF16, align_bytes=64)
        lam = keep.tile([P, 2], BF16)
        x_codes = keep.tile([P, M_TILES, PASSES * P], U32, align_bytes=64)
        x_scales = keep.tile([P, M_TILES, PASSES * P], U8, align_bytes=64)
        w_codes = keep.tile([P, 6, PASSES, N_TILE], U32, align_bytes=64)
        w_scales = keep.tile([P, 6, PASSES, N_TILE], U8, align_bytes=64)
        v_res = keep.tile([P, M_TILES, 2, N_TILE], F32)

        def load_tokens(dst, tiles, m0, count):
            j0 = m0 % SEQ_TILES
            nc.sync.dma_start(out=dst[:, m0 : m0 + count, :], in_=tiles[:, m0 // SEQ_TILES, j0 : j0 + count, :])

        def load_weights(tile0, count, cols=slice(0, C)):
            nc.sync.dma_start(out=w_raw[:, tile0 : tile0 + count, cols], in_=w_tiles[:, tile0 : tile0 + count, cols])

        for g in range(PASSES):
            load_weights(0, 2, slice(g * K_PASS, (g + 1) * K_PASS))
        load_tokens(x_raw, x_tiles, 0, 1)
        load_weights(2, 2)
        load_tokens(x_raw, x_tiles, 1, 1)
        load_tokens(x_raw, x_tiles, 2, 2)
        nc.sync.dma_start(out=lam[:], in_=lambdas.partition_broadcast(P))
        load_tokens(x_raw, x_tiles, 4, 2)
        load_tokens(x_raw, x_tiles, 6, 2)
        load_weights(Q1 * HEADS, HEADS)
        load_tokens(ve_raw, ve_tiles, 0, SEQ_TILES)
        load_weights(V0 * HEADS, HEADS)
        load_weights(K0 * HEADS, HEADS)
        load_tokens(ve_raw, ve_tiles, SEQ_TILES, SEQ_TILES)
        load_weights(V1 * HEADS, HEADS)
        load_weights(K1 * HEADS, HEADS)

        pos = keep.tile([P, SEQ_TILES], F32)
        nc.gpsimd.iota(pos[:], [[1, SEQ_TILES]], base=0, channel_multiplier=SEQ_TILES, allow_small_or_imprecise_dtypes=True)
        ident = keep.tile([P, P], F32)
        make_identity(nc, ident[:])
        eps = keep.tile([P, 1], F32)
        nc.gpsimd.memset(eps[:], EPS)
        zeros = keep.tile([P, 2 * P], F32)
        nc.vector.memset(zeros[:], 0.0)

        turns = keep.tile([P, ROT, SEQ_TILES], F32)
        ratio = (1.0 / ROPE_BASE) ** (1.0 / (ROT - 1))
        for i in range(4):
            nc.vector.tensor_scalar(out=turns[:, i, :], in0=pos[:], scalar1=ratio ** i / (2.0 * math.pi), scalar2=None,
                                    op0=ALU.mult)
        for i in range(4, ROT, 4):
            nc.vector.tensor_scalar(out=turns[:, i : i + 4, :], in0=turns[:, 0:4, :], scalar1=ratio ** i, scalar2=None,
                                    op0=ALU.mult)
        turns_flat = turns[:].rearrange("p i j -> p (i j)")
        shifts = (0.25, 0.0)
        whole = keep.tile([P, 2, SEQ_TILES * ROT], I32)
        for row in range(2):
            nc.vector.tensor_scalar(out=whole[:, row], in0=turns_flat, scalar1=shifts[row], scalar2=None, op0=ALU.add)
        perm = keep.tile([P, P], F32)
        nc.vector.tensor_copy(out=perm[:].rearrange("p (a b i) -> p a b i", a=2, b=2),
                              in_=ident[:].rearrange("p (b a i) -> p a b i", a=2, b=2))
        frac = keep.tile([P, 2, SEQ_TILES * ROT], F32)
        for row in range(2):
            nc.vector.scalar_tensor_tensor(out=frac[:, row], in0=turns_flat, scalar=shifts[row], in1=whole[:, row],
                                           op0=ALU.add, op1=ALU.subtract)
        frac_flat = frac[:].rearrange("p a c -> p (a c)")
        minus_frac = keep.tile([P, 2, ROT, SEQ_TILES], F32)
        nc.vector.scalar_tensor_tensor(out=minus_frac[:].rearrange("p a i j -> p (a i j)"), in0=frac_flat, scalar=0.5,
                                       in1=frac_flat, op0=ALU.is_gt, op1=ALU.subtract)
        table = keep.tile([P, SEQ_TILES, 4, ROT], F32)
        for place, (row, sign) in enumerate(((0, 1.0), (0, 1.0), (1, -1.0), (1, 1.0))):
            nc.scalar.activation(out=table[:, :, place, :], in_=minus_frac[:, row].rearrange("p i j -> p j i"),
                                 func=ACT.Sin, scale=-sign * 2.0 * math.pi)

        unread = keep.tile([P, 1], F32)
        nc.scalar.activation(out=unread[:], in_=eps[:], func=ACT.Abs_reciprocal_sqrt, scale=1.0 / D, bias=eps[:])

        def warm_up(count):
            bank = new_bank("norm")
            for c in range(count):
                nc.tensor.matmul(out=bank[:, 0 : 2 * P], lhsT=zeros[:, 0:P], rhs=zeros[:], start=True, stop=True)

        def x_part(m0, count):
            return {"banks": [[(x_raw[:, m, :], g) for g in range(PASSES)] for m in range(m0, m0 + count)],
                    "order": ident,
                    "codes": x_codes[:, m0 : m0 + count, :].rearrange("p m c -> p (m c)"),
                    "scales": x_scales[:, m0 : m0 + count, :].rearrange("p m c -> p (m c)")}

        def w_part(n, g, half0=0, count=2):
            cols = slice(half0 * 2 * P, (half0 + count) * 2 * P)
            return {"banks": [[(w_raw[:, n * HEADS + 2 * half + r, :], g) for r in range(2)]
                              for half in range(half0, half0 + count)],
                    "order": ident if n >= V0 else perm,
                    "codes": w_codes[:, n, g, cols],
                    "scales": w_scales[:, n, g, cols]}

        def transpose_part(part):
            banks = []
            for pieces in part["banks"]:
                bank = new_bank("short")
                for s, (rows, g) in enumerate(pieces):
                    words = rows.bitcast(F32)
                    for u in range(2):
                        nc.tensor.transpose(bank[:, (2 * s + u) * P : (2 * s + u + 1) * P],
                                            words[:, 2 * P * g + u : 2 * P * (g + 1) : 2], part["order"][:])
                banks.append(bank)
            return banks

        def new_staging():
            staging = work.tile([P, 2, 2 * N_TILE], BF16, align_bytes=64, tag="staging")
            return staging

        def copy_bank(staging, j, bank, on_scalar):
            dst = staging[:, j, :].bitcast(F32).rearrange("p (s c u) -> p s c u", s=2, u=2)
            src = bank[:].rearrange("p (s u c) -> p s c u", s=2, u=2)
            if on_scalar:
                nc.scalar.copy(out=dst, in_=src)
            else:
                nc.vector.tensor_copy(out=dst, in_=src)

        def quantize_part(part, staging):
            nc.vector.quantize_mx(out=part["codes"].bitcast(E5M2X4), scales=part["scales"],
                                  in_=staging[:, 0 : len(part["banks"]), :].rearrange("p j c -> p (j c)"))

        def multiply(n, m):
            bank = new_bank("short" if n >= V0 else "norm")
            for g in range(PASSES):
                cols = slice(g * P, (g + 1) * P)
                nc.tensor.matmul_mx(out=bank[:], lhsT=x_codes[:, m, cols].bitcast(E5M2X4), lhsT_scale=x_scales[:, m, cols],
                                    rhs=w_codes[:, n, g, :].bitcast(E5M2X4), rhs_scale=w_scales[:, n, g, :],
                                    start=(g == 0), stop=(g == PASSES - 1))
            return bank

        def store(n, m0, count, src):
            cols = slice((n % 2) * N_TILE, (n % 2 + 1) * N_TILE)
            j0 = m0 % SEQ_TILES
            nc.sync.dma_start(out=outs[n // 2][:, m0 // SEQ_TILES, j0 : j0 + count, cols], in_=src)

        def sum_squares(job, heads):
            for h in heads:
                nc.scalar.activation(out=job["squares"][:, h * D : (h + 1) * D], in_=job["bank"][:, h * D : (h + 1) * D],
                                     func=ACT.Square, accum_out=job["sums"][:, h : h + 1])

        def inverse_rms(job):
            nc.scalar.activation(out=job["rstd"][:], in_=job["sums"][:], func=ACT.Abs_reciprocal_sqrt, scale=1.0 / D,
                                 bias=eps[:])

        def plain_half(job, on_scalar):
            dst = job["result"][:, job["r"], :].rearrange("p (h a b i) -> p h a b i", h=HEADS, a=2, b=2)[:, :, :, 1, :]
            src = job["bank"][:].rearrange("p (h a b i) -> p h a b i", h=HEADS, a=2, b=2)[:, :, 1, :, :]
            if on_scalar:
                for h in range(HEADS):
                    nc.scalar.activation(out=dst[:, h], in_=src[:, h], func=ACT.Copy, scale=job["rstd"][:, h : h + 1])
            else:
                scale = job["rstd"][:].rearrange("p (h a i) -> p h a i", a=1, i=1).to_broadcast([P, HEADS, 2, ROT])
                nc.vector.tensor_tensor(out=dst, in0=src, in1=scale, op=ALU.mult)

        def rope_products(job):
            factors = table[:, job["m"] % SEQ_TILES].rearrange("p (a b) i -> p a (b i)", a=2)
            for h in range(HEADS):
                src = job["bank"][:, h * D : h * D + 2 * ROT].rearrange("p (a i) -> p a i", a=1).to_broadcast([P, 2, 2 * ROT])
                nc.vector.scalar_tensor_tensor(
                    out=job["terms"][:, job["r"] * HEADS + h, :].rearrange("p (a i) -> p a i", a=2), in0=src,
                    scalar=job["rstd"][:, h : h + 1], in1=factors, op0=ALU.mult, op1=ALU.mult)

        def rope_sums(engine, job, r0, count):
            heads = slice(r0 * HEADS, (r0 + count) * HEADS)
            dst = job["result"][:].rearrange("p r (h d) -> p (r h) d", d=D)
            terms = job["terms"]
            engine.tensor_tensor(out=dst[:, heads, 0:ROT], in0=terms[:, heads, 0:ROT], in1=terms[:, heads, 3 * ROT : 4 * ROT],
                                 op=ALU.add)
            engine.tensor_tensor(out=dst[:, heads, 2 * ROT : 3 * ROT], in0=terms[:, heads, ROT : 2 * ROT],
                                 in1=terms[:, heads, 2 * ROT : 3 * ROT], op=ALU.add)
            store(job["n"], job["m"] - job["r"] + r0, count, job["result"][:, r0 : r0 + count, :])

        def scale_ve(n, m):
            nc.gpsimd.tensor_scalar(out=v_res[:, m, n % 2, :], in0=ve_raw[:, m, (n % 2) * N_TILE : (n % 2 + 1) * N_TILE],
                                    scalar1=lam[:, 1:2], scalar2=0.0, op0=ALU.mult, op1=ALU.add)

        def blend(n, m, bank):
            nc.vector.scalar_tensor_tensor(out=v_res[:, m, n % 2, :], in0=bank[:], scalar=lam[:, 0:1],
                                           in1=v_res[:, m, n % 2, :], op0=ALU.mult, op1=ALU.add)
            if m % 2 == 1:
                store(n, m - 1, 2, v_res[:, m - 1 : m + 1, n % 2, :])

        parts_left = [x_part(4, 2), x_part(6, 2)] + [w_part(n, g) for n in (Q1, V0, K0, V1, K1) for g in range(PASSES)]
        v_left = [(n, m) for n in (V0, V1) for m in range(M_TILES)]
        ve_left = list(v_left)
        staged = []

        def take(items, count):
            taken = items[0:count]
            for item in taken:
                items.remove(item)
            return taken

        def finish(job):
            step, second = job["step"], job["r"] == 1
            on_scalar = job["no_copies"] and not (second and step == STEPS - 1)
            if on_scalar:
                plain_half(job, True)
            rope_products(job)
            if second:
                for part, staging in take(staged, len(staged)):
                    quantize_part(part, staging)
            if not on_scalar:
                plain_half(job, False)
            if step >= STEPS - 2:
                rope_sums(nc.vector if step == STEPS - 1 else nc.gpsimd, job, job["r"], 1)
            elif second:
                rope_sums(nc.gpsimd, job, 0, 2)
            if second:
                for n, m in take(ve_left, 2 if step < DOUBLE_SCALE_STEPS else 1):
                    scale_ve(n, m)

        head = ([w_part(Q0, g, 0, 1) for g in range(PASSES)] + [x_part(0, 1)]
                + [w_part(Q0, g, 1, 1) for g in range(PASSES)] + [x_part(m, 1) for m in (1, 2, 3)])
        warm_ups = {0: 3, 3: 1, 5: 1}
        for j, part in enumerate(head):
            if j in warm_ups:
                warm_up(warm_ups[j])
            staging = new_staging()
            copy_bank(staging, 0, transpose_part(part)[0], j % 2 == 1)
            for earlier in take(staged, 1):
                quantize_part(*earlier)
            staged.append((part, staging))
        quantize_part(*take(staged, 1)[0])

        pending = None
        pairs = [(n, m0) for n in (Q0, Q1, K0, K1) for m0 in range(0, M_TILES, 2)]
        for step, (n, m0) in enumerate(pairs):
            parts = take(parts_left, 2 if step in DOUBLE_PART_STEPS else 1)
            v_tiles = take(v_left, 0 if step < V_FIRST else 1 if step < V_DOUBLE else 2)
            result = res.tile([P, 2, N_TILE], F32, name="result", tag="result")
            terms = work.tile([P, 2 * HEADS, D], F32, tag="terms", bufs=3)
            jobs = []
            for r in range(2):
                squares = work.tile([P, N_TILE], F32, tag="squares", bufs=2)
                sums = work.tile([P, HEADS], F32, tag="sums")
                rstd = work.tile([P, HEADS], F32, tag="rstd")
                jobs.append({"step": step, "n": n, "m": m0 + r, "r": r, "no_copies": not parts, "result": result,
                             "terms": terms, "squares": squares, "sums": sums, "rstd": rstd, "bank": multiply(n, m0 + r)})
            v_banks = [multiply(*v) for v in v_tiles]
            for job in jobs:
                sum_squares(job, range(0, 2))
                if pending is not None:
                    inverse_rms(pending)
                sum_squares(job, range(2, HEADS))
                if pending is not None:
                    finish(pending)
                pending = job
            for v, bank in zip(v_tiles, v_banks):
                blend(v[0], v[1], bank)
            part_banks = [transpose_part(part) for part in parts]
            copies = 0
            for part, banks in zip(parts, part_banks):
                staging = new_staging()
                for j, bank in enumerate(banks):
                    copy_bank(staging, j, bank, copies < SCALAR_COPIES)
                    if copies == 0:
                        inverse_rms(pending)
                    copies += 1
                staged.append((part, staging))
            if parts:
                finish(pending)
                pending = None
        inverse_rms(pending)
        finish(pending)
